import numpy as np
import ml_dtypes


def mxq(x, axis, fmt="e4m3"):
    dtype, down = {"e4m3": (ml_dtypes.float8_e4m3fn, 7), "e5m2": (ml_dtypes.float8_e5m2, 14)}[fmt]
    v = np.moveaxis(np.asarray(x, np.float32).astype(ml_dtypes.bfloat16).astype(np.float64), axis, -1)
    blocks = v.reshape(v.shape[:-1] + (-1, 32))
    amax = np.abs(blocks).max(-1, keepdims=True)
    byte = np.maximum(np.where(amax > 0, np.frexp(amax)[1] - 1 + 127, 0) - down, 1)
    scale = np.exp2(byte - 127.0)
    codes = (blocks / scale).astype(np.float32).astype(dtype).astype(np.float64)
    return np.moveaxis((codes * scale).reshape(v.shape), -1, axis)


WIDE = False


def mx_kscale(k):
    if not WIDE:
        return np.ones(k)
    levels = np.array([10, -10, 5, -5, 0])
    if k % 512:
        return np.exp2(np.random.permutation(np.resize(levels, k // 32))).repeat(32)
    a = np.empty((k // 512, 16))
    for p in range(k // 512):
        a[p, :8] = np.random.permutation(np.resize(levels, 8))
        for g in range(8):
            far = levels[np.abs(levels - a[p, g]) >= 10]
            a[p, g + 8] = far[np.random.randint(len(far))]
    return np.exp2(a.ravel()).repeat(32)


BF16 = ml_dtypes.bfloat16


def bf(x):
    return np.asarray(x, np.float32).astype(BF16)


def f64(x):
    return np.asarray(x).astype(np.float64)


T, H, QR, NH, DN, DR, KVR = 512, 2048, 1536, 16, 128, 64, 448
EPS = 1e-6


def rmsnorm(x, gamma):
    var = np.mean(np.square(x), axis=-1, keepdims=True)
    return x * (1.0 / np.sqrt(var + EPS)) * gamma


def apply_rope(x, cos, sin):
    x1, x2 = np.split(x, 2, axis=-1)
    rot = np.concatenate([-x2, x1], axis=-1)
    return x * cos + rot * sin


def setup_inputs():
    s, t = mx_kscale(H), mx_kscale(QR)
    return {"token_x": bf(np.random.standard_normal((T, H)) * s),
            "wq_a": bf(np.random.standard_normal((H, QR)) / np.sqrt(H) / s[:, None]),
            "wq_b": bf(np.random.standard_normal((QR, NH * (DN + DR))) / np.sqrt(QR) / t[:, None]),
            "wkv": bf(np.random.standard_normal((H, KVR + DR)) / np.sqrt(H) / s[:, None]),
            "rope_cos": bf(np.random.uniform(-1.0, 1.0, (T, DR))),
            "rope_sin": bf(np.random.uniform(-1.0, 1.0, (T, DR))),
            "gamma_cq": bf((1.0 + 0.1 * np.random.standard_normal(QR)) * t),
            "gamma_ckv": bf(1.0 + 0.1 * np.random.standard_normal(KVR))}


def reference(token_x, wq_a, wq_b, wkv, rope_cos, rope_sin, gamma_cq, gamma_ckv):
    cos, sin = f64(rope_cos), f64(rope_sin)
    xq = mxq(f64(token_x), 1, "e4m3")
    cq = rmsnorm(xq @ mxq(f64(wq_a), 0, "e4m3"), f64(gamma_cq))
    q = (mxq(cq, 1, "e4m3") @ mxq(f64(wq_b), 0, "e4m3")).reshape(T, NH, DN + DR)
    q_nope, q_rope = q[..., :DN], q[..., DN:]
    q_rope = apply_rope(q_rope, cos[:, None, :], sin[:, None, :])
    query = np.concatenate([q_nope, q_rope], axis=-1)
    kv = xq @ mxq(f64(wkv), 0, "e4m3")
    ckv = rmsnorm(kv[:, :KVR], f64(gamma_ckv))
    k_rope = apply_rope(kv[:, KVR:], cos, sin)
    return np.concatenate([query.reshape(T, -1), ckv, k_rope], axis=-1)

@@ -1,0 +1,496 @@
+from contextlib import ExitStack
+
+import concourse.mybir as mybir
+from concourse.masks import make_identity
+
+F32 = mybir.dt.float32
+BF16 = mybir.dt.bfloat16
+U32 = mybir.dt.uint32
+U8 = mybir.dt.uint8
+FP8X4 = mybir.dt.float8_e4m3fn_x4
+ALU = mybir.AluOpType
+ACT = mybir.ActivationFunctionType
+
+P = 128
+TILES = 4
+T, H, QR, NQ, KV, KVR, DR = 512, 2048, 1536, 3072, 512, 448, 64
+HALF = DR // 2
+W = 512
+EPS = 1e-6
+FLOPS = 2 * T * (H * QR + QR * NQ + H * KV)
+
+EARLY_BANKS = ((0, 0), (0, 1), (0, 2), (1, 0), (1, 1), (1, 2), (2, 0), (2, 1))
+
+COPY_ENGINE = "VSVV" + "VSVSVSVSVSVS" + "SVSSVSSVSSVSSVSSVV"
+CQ_COPY_ENGINE = "SSSSVV"
+
+FIRST_ROPE_SLOT = (2, 0, 1)
+KV_ROPE_SLOT = 7
+
+
+def tile_mla_model_kernel(
+    tc, token_x, wq_a, wq_b, wkv, rope_cos, rope_sin, gamma_cq, gamma_ckv, out
+):
+    nc = tc.nc
+    with ExitStack() as ctx:
+        const = ctx.enter_context(tc.tile_pool(name="const", bufs=1))
+        keep = ctx.enter_context(tc.tile_pool(name="keep", bufs=1))
+        raw_pool = ctx.enter_context(tc.tile_pool(name="raw", bufs=6))
+        code_pool = ctx.enter_context(tc.tile_pool(name="codes", bufs=6))
+        small_raw = ctx.enter_context(tc.tile_pool(name="small_raw", bufs=5))
+        grouped_pool = ctx.enter_context(tc.tile_pool(name="grouped", bufs=6))
+        rope_pool = ctx.enter_context(tc.tile_pool(name="rope", bufs=3))
+        junk_pool = ctx.enter_context(tc.tile_pool(name="junk", bufs=2))
+        cqg_pool = ctx.enter_context(tc.tile_pool(name="cqg", bufs=4))
+        cq_pool = ctx.enter_context(tc.tile_pool(name="cq", bufs=3))
+        stat = ctx.enter_context(tc.tile_pool(name="stat", bufs=4))
+        out_pool = ctx.enter_context(tc.tile_pool(name="outp", bufs=7))
+        psum = ctx.enter_context(tc.psum_pool(name="psum", bufs=8))
+
+        x_view = token_x.rearrange("(p t) h -> p t h", t=TILES)
+        out_view = out.rearrange("(p t) n -> p t n", t=TILES)
+
+        eps = const.tile([P, 1], F32, name="eps")
+        nc.vector.memset(eps[:], EPS)
+        gain_rows = grouped_pool.tile([P, 4 * W], BF16, tag="grouped", name="gain_rows", align_bytes=64)
+        nc.vector.memset(gain_rows[:], 0.0)
+        ones = const.tile([P, P], BF16, name="ones")
+        nc.vector.memset(ones[:], 1.0)
+        cos_raw = const.tile([P, TILES, DR], BF16, name="cos_raw")
+        sin_raw = const.tile([P, TILES, DR], BF16, name="sin_raw")
+        warm = const.tile([P, 1], F32, name="warm")
+        nc.scalar.activation(out=warm[:], in_=eps[:], func=ACT.Sqrt)
+        ident_f32 = const.tile([P, P], F32, name="ident_f32")
+        make_identity(nc, ident_f32[:])
+        ident_bf16 = const.tile([P, P], BF16, name="ident_bf16")
+        make_identity(nc, ident_bf16[:])
+
+        x_raw = []
+        wkv_raw = []
+
+        def load_x(t, pieces):
+            x_raw.append(small_raw.tile([P, H], BF16, tag="small", name="x_raw%d" % t))
+            wid = H // pieces
+            for i in range(pieces):
+                nc.sync.dma_start(out=x_raw[t][:, wid * i:wid * i + wid], in_=x_view[:, t, wid * i:wid * i + wid])
+
+        def load_wkv(g):
+            chunk = small_raw.tile([P, 4, W], BF16, tag="small", name="wkv_raw%d" % g)
+            nc.sync.dma_start(
+                out=chunk[:],
+                in_=wkv[512 * g:512 * g + 512, :].rearrange("(p j) c -> p j c", j=4),
+            )
+            wkv_raw.append(chunk)
+
+        load_x(0, 2)
+        load_x(1, 1)
+        nc.sync.dma_start(out=gain_rows[0:1, 0:QR], in_=gamma_cq.unsqueeze(0))
+        nc.sync.dma_start(out=gain_rows[0:1, QR:QR + KVR], in_=gamma_ckv.unsqueeze(0))
+        nc.sync.dma_start(out=cos_raw[:], in_=rope_cos.rearrange("(p t) d -> p t d", t=TILES))
+        nc.sync.dma_start(out=sin_raw[:], in_=rope_sin.rearrange("(p t) d -> p t d", t=TILES))
+        load_wkv(0)
+        load_x(2, 1)
+        load_wkv(1)
+        load_x(3, 1)
+        load_wkv(2)
+        load_wkv(3)
+
+        table_1 = const.tile([P, TILES, DR], F32, name="table_1")
+        table_2 = const.tile([P, TILES, DR], F32, name="table_2")
+        nc.gpsimd.tensor_copy(out=table_1[:, :, 0:HALF], in_=cos_raw[:, :, 0:HALF])
+        nc.gpsimd.tensor_copy(out=table_1[:, :, HALF:DR], in_=sin_raw[:, :, HALF:DR])
+        nc.gpsimd.tensor_scalar(
+            out=table_2[:, :, 0:HALF], in0=sin_raw[:, :, 0:HALF], scalar1=-1.0, scalar2=0.0,
+            op0=ALU.mult, op1=ALU.add,
+        )
+        nc.gpsimd.tensor_copy(out=table_2[:, :, HALF:DR], in_=cos_raw[:, :, HALF:DR])
+
+        x_codes = keep.tile([P, TILES, W], U32, name="x_codes", align_bytes=64)
+        x_scales = keep.tile([P, TILES, W], U8, name="x_scales", align_bytes=64)
+        wkv_codes = keep.tile([P, 4, W], U32, name="wkv_codes", align_bytes=64)
+        wkv_scales = keep.tile([P, 4, W], U8, name="wkv_scales", align_bytes=64)
+        cq_codes = keep.tile([P, TILES, 3 * P], U32, name="cq_codes", align_bytes=64)
+        cq_scales = keep.tile([P, TILES, 3 * P], U8, name="cq_scales", align_bytes=64)
+        gain_q = const.tile([P, QR], BF16, name="gain_q")
+        gain_kv = const.tile([P, W], BF16, name="gain_kv")
+
+        units = []
+        for g in range(4):
+            units.append((wkv_raw[g][:], wkv_codes[:, g, :], wkv_scales[:, g, :], None))
+        wa_codes, wa_scales = [], []
+        for g in range(4):
+            chunk = raw_pool.tile([P, 4, QR], BF16, tag="raw", name="wa_raw%d" % g)
+            if g == 0:
+                for c in range(3):
+                    nc.sync.dma_start(
+                        out=chunk[:, :, W * c:W * c + W],
+                        in_=wq_a[0:512, W * c:W * c + W].rearrange("(p j) c -> p j c", j=4),
+                    )
+            else:
+                nc.sync.dma_start(
+                    out=chunk[:],
+                    in_=wq_a[512 * g:512 * g + 512, :].rearrange("(p j) c -> p j c", j=4),
+                )
+            wa_codes.append(code_pool.tile([P, QR], U32, tag="codes", name="wa_codes%d" % g, align_bytes=64))
+            wa_scales.append(code_pool.tile([P, QR], U8, tag="scales", name="wa_scales%d" % g, align_bytes=64))
+            for c in range(3):
+                cols = slice(W * c, W * c + W)
+                units.append((chunk[:, :, cols], wa_codes[g][:, cols], wa_scales[g][:, cols], ("a", g, c)))
+        wb_codes, wb_scales = {}, {}
+        for half in range(2):
+            chunks = []
+            for g in range(3):
+                chunk = raw_pool.tile([P, 4, QR], BF16, tag="raw", name="wb_raw%d%d" % (half, g))
+                nc.sync.dma_start(
+                    out=chunk[:],
+                    in_=wq_b[512 * g:512 * g + 512, QR * half:QR * half + QR].rearrange("(p j) n -> p j n", j=4),
+                )
+                chunks.append(chunk)
+                wb_codes[(half, g)] = code_pool.tile(
+                    [P, QR], U32, tag="codes", name="wb_codes%d%d" % (half, g), align_bytes=64
+                )
+                wb_scales[(half, g)] = code_pool.tile(
+                    [P, QR], U8, tag="scales", name="wb_scales%d%d" % (half, g), align_bytes=64
+                )
+            for c in range(3):
+                cols = slice(W * c, W * c + W)
+                for g in range(3):
+                    units.append((
+                        chunks[g][:, :, cols], wb_codes[(half, g)][:, cols], wb_scales[(half, g)][:, cols],
+                        ("q", 3 * half + c, g),
+                    ))
+
+        a_bank = {}
+        q_bank = {}
+        grouped = {}
+        done = {"copied": 0, "quantised": 0, "multiplied": 0}
+
+        def stage1_pass(t, c, g):
+            cols = slice(W * c, W * c + W)
+            nc.tensor.matmul_mx(
+                out=a_bank[(t, c)][:],
+                lhsT=x_codes[:, t, P * g:P * g + P].bitcast(FP8X4),
+                lhsT_scale=x_scales[:, t, P * g:P * g + P],
+                rhs=wa_codes[g][:, cols].bitcast(FP8X4),
+                rhs_scale=wa_scales[g][:, cols],
+                start=(g == 0),
+                stop=(g == 3),
+            )
+
+        def regroup_next():
+            k = done["copied"]
+            if k >= len(units):
+                return
+            done["copied"] = k + 1
+            grouped[k] = grouped_pool.tile([P, 4 * W], BF16, tag="grouped", name="grouped%d" % k, align_bytes=64)
+            dst = grouped[k][:].rearrange("p (c i t) -> p c t i", i=4, t=4)
+            src = units[k][0].rearrange("p t (c i) -> p c t i", i=4)
+            if COPY_ENGINE[k] == "S":
+                nc.scalar.copy(out=dst, in_=src)
+            else:
+                nc.vector.tensor_copy(out=dst, in_=src)
+
+        def quantise_next():
+            k = done["quantised"]
+            if k >= len(units):
+                return
+            done["quantised"] = k + 1
+            nc.vector.quantize_mx(out=units[k][1].bitcast(FP8X4), scales=units[k][2], in_=grouped[k][:])
+
+        def multiply_next():
+            k = done["multiplied"]
+            if k >= len(units):
+                return
+            done["multiplied"] = k + 1
+            what = units[k][3]
+            if what is None:
+                return
+            if what[0] == "a":
+                g, c = what[1], what[2]
+                for t in range(TILES):
+                    if (t, c) in EARLY_BANKS:
+                        if g == 0:
+                            a_bank[(t, c)] = psum.tile([P, W], F32, tag="bank", name="a%d%d" % (t, c))
+                        stage1_pass(t, c, g)
+            else:
+                s, g = what[1], what[2]
+                half, c = divmod(s, 3)
+                cols = slice(W * c, W * c + W)
+                for t in range(TILES):
+                    if g == 0:
+                        q_bank[(s, t)] = psum.tile([P, W], F32, tag="bank", name="q%d%d" % (s, t))
+                    nc.tensor.matmul_mx(
+                        out=q_bank[(s, t)][:],
+                        lhsT=cq_codes[:, t, P * g:P * g + P].bitcast(FP8X4),
+                        lhsT_scale=cq_scales[:, t, P * g:P * g + P],
+                        rhs=wb_codes[(half, g)][:, cols].bitcast(FP8X4),
+                        rhs_scale=wb_scales[(half, g)][:, cols],
+                        start=(g == 0),
+                        stop=(g == 2),
+                    )
+
+        def advance():
+            regroup_next()
+            quantise_next()
+            multiply_next()
+
+        x_grouped = {}
+        x_bank = {}
+
+        def x_transpose(t):
+            words = x_raw[t][:].bitcast(F32)
+            x_grouped[t] = grouped_pool.tile([P, 4 * W], BF16, tag="grouped", name="x_grouped%d" % t, align_bytes=64)
+            for pair in range(2):
+                x_bank[(t, pair)] = psum.tile([P, 4, P], F32, tag="bank", name="x_bank%d%d" % (t, pair))
+                for i in range(4):
+                    g, u = divmod(i, 2)
+                    w0 = W * pair + 2 * P * g
+                    nc.tensor.transpose(
+                        out=x_bank[(t, pair)][:, i, :], in_=words[:, w0 + u:w0 + 2 * P:2], identity=ident_f32[:]
+                    )
+            for pair in range(2):
+                dst = x_grouped[t][:].bitcast(F32)[:, W * pair:W * pair + W].rearrange("p (g r u) -> p g r u", g=2, u=2)
+                nc.scalar.copy(out=dst, in_=x_bank[(t, pair)][:].rearrange("p (g u) r -> p g r u", u=2))
+
+        def x_quantise(t):
+            nc.vector.quantize_mx(out=x_codes[:, t, :].bitcast(FP8X4), scales=x_scales[:, t, :], in_=x_grouped[t][:])
+
+        def spread_gains(c):
+            bank = psum.tile([P, W], F32, tag="bank", name="gain_bank%d" % c)
+            nc.tensor.matmul(out=bank[:], lhsT=ones[:], rhs=gain_rows[:, W * c:W * c + W], start=True, stop=True)
+            if c < 3:
+                nc.scalar.copy(
+                    out=gain_q[:, W * c:W * c + W].rearrange("r (j p) -> r j p", j=4),
+                    in_=bank[:].rearrange("r (p j) -> r j p", j=4),
+                )
+            else:
+                nc.scalar.copy(out=gain_kv[:], in_=bank[:])
+
+        cq = {}
+        sums = {}
+        rms = {}
+        cq_bank = {}
+        cq_grouped = {}
+        cq_codes_flat = cq_codes[:].rearrange("p t w -> p (t w)")
+        cq_scales_flat = cq_scales[:].rearrange("p t w -> p (t w)")
+
+        def squares(t, thirds):
+            if t not in sums:
+                sums[t] = stat.tile([P, 4], F32, tag="sums", name="sums%d" % t)
+            for c in thirds:
+                junk = junk_pool.tile([P, W], BF16, tag="junk", name="junk")
+                nc.scalar.activation(
+                    out=junk[:], in_=a_bank[(t, c)][:], func=ACT.Square, accum_out=sums[t][:, c:c + 1]
+                )
+
+        def root_mean_square(t):
+            total = stat.tile([P, 1], F32, tag="total", name="total%d" % t)
+            copy3 = stat.tile([P, 4], F32, tag="copy3", name="copy3")
+            nc.scalar.activation(out=copy3[:, 0:3], in_=sums[t][:, 0:3], func=ACT.Copy, accum_out=total[:])
+            rms[t] = stat.tile([P, 1], F32, tag="rms", name="rms%d" % t)
+            nc.scalar.activation(out=rms[t][:], in_=total[:], func=ACT.Sqrt, bias=eps[:, 0:1], scale=1.0 / QR)
+
+        def scale_cq(t):
+            rstd = stat.tile([P, 1], F32, tag="rstd", name="rstd%d" % t)
+            nc.vector.reciprocal(out=rstd[:], in_=rms[t][:])
+            cq[t] = cq_pool.tile([P, QR], BF16, tag="cq", name="cq%d" % t)
+            for c in range(3):
+                cols = slice(W * c, W * c + W)
+                nc.vector.scalar_tensor_tensor(
+                    out=cq[t][:, cols].rearrange("r (j p) -> r j p", j=4),
+                    in0=a_bank[(t, c)][:].rearrange("r (p j) -> r j p", j=4),
+                    scalar=rstd[:, 0:1],
+                    in1=gain_q[:, cols].rearrange("r (j p) -> r j p", j=4),
+                    op0=ALU.mult, op1=ALU.mult,
+                )
+
+        def late_bank(t, c):
+            a_bank[(t, c)] = psum.tile([P, W], F32, tag="bank", name="a%d%d" % (t, c))
+            for g in range(4):
+                stage1_pass(t, c, g)
+
+        def cq_transpose(pair):
+            cq_bank[pair] = psum.tile([P, 8, P], BF16, tag="bank", name="cq_bank%d" % pair)
+            for h in range(2):
+                t, g = divmod(2 * pair + h, 3)
+                for j in range(4):
+                    k0 = 512 * g + P * j
+                    nc.tensor.transpose(
+                        out=cq_bank[pair][:, 4 * h + j, :], in_=cq[t][:, k0:k0 + P], identity=ident_bf16[:]
+                    )
+
+        def cq_copy(pair):
+            cq_grouped[pair] = cqg_pool.tile([P, 2 * W], BF16, tag="cqg", name="cq_grouped%d" % pair, align_bytes=64)
+            dst = cq_grouped[pair][:].rearrange("p (h r j) -> p h r j", h=2, j=4)
+            src = cq_bank[pair][:].rearrange("p (h j) r -> p h r j", h=2)
+            if CQ_COPY_ENGINE[pair] == "S":
+                nc.scalar.copy(out=dst, in_=src)
+            else:
+                nc.vector.tensor_copy(out=dst, in_=src)
+
+        def cq_quantise(pair):
+            nc.vector.quantize_mx(
+                out=cq_codes_flat[:, 2 * P * pair:2 * P * pair + 2 * P].bitcast(FP8X4),
+                scales=cq_scales_flat[:, 2 * P * pair:2 * P * pair + 2 * P],
+                in_=cq_grouped[pair][:],
+            )
+
+        products = {}
+        out_tile = {}
+
+        def rope_products(key, bank, first_slot, t):
+            n = len(range(first_slot, 8, 3))
+            halves = bank[:].rearrange("p (s w) -> p s w", w=HALF)
+            shape = [P, n, 2, HALF]
+            x1 = halves[:, 2 * first_slot:16:6, :].unsqueeze(2).to_broadcast(shape)
+            x2 = halves[:, 2 * first_slot + 1:16:6, :].unsqueeze(2).to_broadcast(shape)
+            t1 = table_1[:, t, :].rearrange("p (h w) -> p h w", h=2).unsqueeze(1).to_broadcast(shape)
+            t2 = table_2[:, t, :].rearrange("p (h w) -> p h w", h=2).unsqueeze(1).to_broadcast(shape)
+            p1 = rope_pool.tile([P, 3, 2, HALF], F32, tag="p1", name="p1")
+            p2 = rope_pool.tile([P, 3, 2, HALF], F32, tag="p2", name="p2")
+            nc.vector.tensor_tensor(out=p1[:, 0:n], in0=x1, in1=t1, op=ALU.mult)
+            nc.vector.tensor_tensor(out=p2[:, 0:n], in0=x2, in1=t2, op=ALU.mult)
+            products[key] = (p1, p2, n, first_slot)
+
+        def rope_sum(key):
+            p1, p2, n, first_slot = products[key]
+            slots = out_tile[key][:].rearrange("p (s h w) -> p s h w", h=2, w=HALF)
+            nc.vector.tensor_tensor(out=slots[:, first_slot:8:3], in0=p1[:, 0:n], in1=p2[:, 0:n], op=ALU.add)
+
+        kv_bank = {}
+        kv_rms = {}
+
+        def kv_passes(t):
+            kv_bank[t] = psum.tile([P, W], F32, tag="bank", name="kv%d" % t)
+            for g in range(4):
+                nc.tensor.matmul_mx(
+                    out=kv_bank[t][:],
+                    lhsT=x_codes[:, t, P * g:P * g + P].bitcast(FP8X4),
+                    lhsT_scale=x_scales[:, t, P * g:P * g + P],
+                    rhs=wkv_codes[:, g, :].bitcast(FP8X4),
+                    rhs_scale=wkv_scales[:, g, :],
+                    start=(g == 0),
+                    stop=(g == 3),
+                )
+
+        def kv_root_mean_square(t):
+            total = stat.tile([P, 1], F32, tag="total", name="kv_total%d" % t)
+            junk = junk_pool.tile([P, W], BF16, tag="junk", name="junk")
+            nc.scalar.activation(out=junk[:, 0:KVR], in_=kv_bank[t][:, 0:KVR], func=ACT.Square, accum_out=total[:])
+            kv_rms[t] = stat.tile([P, 1], F32, tag="rms", name="kv_rms%d" % t)
+            nc.scalar.activation(out=kv_rms[t][:], in_=total[:], func=ACT.Sqrt, bias=eps[:, 0:1], scale=1.0 / KVR)
+
+        def kv_finish(t):
+            rstd = stat.tile([P, 1], F32, tag="rstd", name="kv_rstd%d" % t)
+            nc.vector.reciprocal(out=rstd[:], in_=kv_rms[t][:])
+            out_tile[("kv", t)] = out_pool.tile([P, W], F32, tag="out", name="kv_out%d" % t)
+            nc.vector.scalar_tensor_tensor(
+                out=out_tile[("kv", t)][:, 0:KVR], in0=kv_bank[t][:, 0:KVR], scalar=rstd[:, 0:1],
+                in1=gain_kv[:, 0:KVR], op0=ALU.mult, op1=ALU.mult,
+            )
+            rope_products(("kv", t), kv_bank[t], KV_ROPE_SLOT, t)
+            rope_sum(("kv", t))
+            nc.sync.dma_start(out=out_view[:, t, NQ:NQ + KV], in_=out_tile[("kv", t)][:])
+
+        def plain_columns_out(s, t):
+            rope_class = FIRST_ROPE_SLOT[s % 3] % 3
+            out_tile[(s, t)] = out_pool.tile([P, W], F32, tag="out", name="q_out%d%d" % (s, t))
+            src = q_bank[(s, t)][:].rearrange("p (s w) -> p s w", w=DR)
+            dst = out_tile[(s, t)][:].rearrange("p (s w) -> p s w", w=DR)
+            for r in range(3):
+                if r != rope_class:
+                    nc.scalar.copy(out=dst[:, r:8:3, :], in_=src[:, r:8:3, :])
+
+        def q_store(s, t):
+            rope_sum((s, t))
+            nc.sync.dma_start(out=out_view[:, t, W * s:W * s + W], in_=out_tile[(s, t)][:])
+
+        x_transpose(0)
+        x_transpose(1)
+        x_quantise(0)
+        regroup_next()
+        x_transpose(2)
+        x_quantise(1)
+        regroup_next()
+        quantise_next()
+        multiply_next()
+        x_transpose(3)
+        x_quantise(2)
+        advance()
+        x_quantise(3)
+        for c in (3, 0, 1, 2):
+            spread_gains(c)
+        advance()
+        advance()
+        for t in range(TILES):
+            kv_passes(t)
+        advance()
+        kv_root_mean_square(0)
+        kv_root_mean_square(1)
+        advance()
+        kv_root_mean_square(2)
+        kv_finish(0)
+        advance()
+        kv_root_mean_square(3)
+        kv_finish(1)
+        advance()
+        kv_finish(2)
+        advance()
+        kv_finish(3)
+
+        regroup_next()
+        for k in range(7):
+            advance()
+
+        squares(0, (0, 1, 2))
+        root_mean_square(0)
+        quantise_next()
+        squares(1, (0, 1, 2))
+        root_mean_square(1)
+        scale_cq(0)
+        late_bank(2, 2)
+        late_bank(3, 0)
+        late_bank(3, 1)
+        squares(2, (0, 1))
+        scale_cq(1)
+        late_bank(3, 2)
+        squares(2, (2,))
+        root_mean_square(2)
+        cq_transpose(0)
+        squares(3, (0,))
+        scale_cq(2)
+        squares(3, (1, 2))
+        root_mean_square(3)
+        cq_transpose(1)
+        cq_transpose(2)
+        cq_copy(0)
+        scale_cq(3)
+        cq_transpose(3)
+        cq_copy(1)
+        cq_quantise(0)
+        cq_transpose(4)
+        cq_transpose(5)
+        cq_copy(2)
+        cq_copy(4)
+        cq_quantise(1)
+        cq_copy(3)
+        cq_copy(5)
+        cq_quantise(2)
+        cq_quantise(4)
+        cq_quantise(3)
+        cq_quantise(5)
+        multiply_next()
+        advance()
+        advance()
+
+        banks = [(s, t) for s in range(6) for t in range(TILES)]
+        for n in range(len(banks) + 2):
+            if n < len(banks):
+                plain_columns_out(*banks[n])
+            if 1 <= n <= len(banks):
+                s, t = banks[n - 1]
+                rope_products((s, t), q_bank[(s, t)], FIRST_ROPE_SLOT[s % 3], t)
+            if n >= 2:
+                q_store(*banks[n - 2])
+            if n % 4 != 3:
+                advance()

@@ -21,7 +21,7 @@ FLOPS = 2 * T * (H * QR + QR * NQ + H * KV)
 
 EARLY_BANKS = ((0, 0), (0, 1), (0, 2), (1, 0), (1, 1), (1, 2), (2, 0), (2, 1))
 
-COPY_ENGINE = "VSVV" + "VSVSVSVSVSVS" + "SVSSVSSVSSVSSVSSVV"
+COPY_ENGINE = "VSVV" + "VSVSVSVSVSVS" + "SVSSVSSVSVVSSVSSVV"
 CQ_COPY_ENGINE = "SSSSVV"
 
 FIRST_ROPE_SLOT = (2, 0, 1)
@@ -62,17 +62,13 @@ def tile_mla_model_kernel(
         nc.scalar.activation(out=warm[:], in_=eps[:], func=ACT.Sqrt)
         ident_f32 = const.tile([P, P], F32, name="ident_f32")
         make_identity(nc, ident_f32[:])
-        ident_bf16 = const.tile([P, P], BF16, name="ident_bf16")
-        make_identity(nc, ident_bf16[:])
 
         x_raw = []
         wkv_raw = []
 
-        def load_x(t, pieces):
+        def load_x(t):
             x_raw.append(small_raw.tile([P, H], BF16, tag="small", name="x_raw%d" % t))
-            wid = H // pieces
-            for i in range(pieces):
-                nc.sync.dma_start(out=x_raw[t][:, wid * i:wid * i + wid], in_=x_view[:, t, wid * i:wid * i + wid])
+            nc.sync.dma_start(out=x_raw[t][:], in_=x_view[:, t, :])
 
         def load_wkv(g):
             chunk = small_raw.tile([P, 4, W], BF16, tag="small", name="wkv_raw%d" % g)
@@ -82,16 +78,16 @@ def tile_mla_model_kernel(
             )
             wkv_raw.append(chunk)
 
-        load_x(0, 2)
-        load_x(1, 1)
+        load_wkv(0)
+        load_x(0)
+        load_x(1)
         nc.sync.dma_start(out=gain_rows[0:1, 0:QR], in_=gamma_cq.unsqueeze(0))
         nc.sync.dma_start(out=gain_rows[0:1, QR:QR + KVR], in_=gamma_ckv.unsqueeze(0))
         nc.sync.dma_start(out=cos_raw[:], in_=rope_cos.rearrange("(p t) d -> p t d", t=TILES))
         nc.sync.dma_start(out=sin_raw[:], in_=rope_sin.rearrange("(p t) d -> p t d", t=TILES))
-        load_wkv(0)
-        load_x(2, 1)
+        load_x(2)
         load_wkv(1)
-        load_x(3, 1)
+        load_x(3)
         load_wkv(2)
         load_wkv(3)
 
@@ -111,8 +107,7 @@ def tile_mla_model_kernel(
         wkv_scales = keep.tile([P, 4, W], U8, name="wkv_scales", align_bytes=64)
         cq_codes = keep.tile([P, TILES, 3 * P], U32, name="cq_codes", align_bytes=64)
         cq_scales = keep.tile([P, TILES, 3 * P], U8, name="cq_scales", align_bytes=64)
-        gain_q = const.tile([P, QR], BF16, name="gain_q")
-        gain_kv = const.tile([P, W], BF16, name="gain_kv")
+        gains = const.tile([P, 4 * W], BF16, name="gains")
 
         units = []
         for g in range(4):
@@ -255,16 +250,15 @@ def tile_mla_model_kernel(
         def x_quantise(t):
             nc.vector.quantize_mx(out=x_codes[:, t, :].bitcast(FP8X4), scales=x_scales[:, t, :], in_=x_grouped[t][:])
 
-        def spread_gains(c):
-            bank = psum.tile([P, W], F32, tag="bank", name="gain_bank%d" % c)
-            nc.tensor.matmul(out=bank[:], lhsT=ones[:], rhs=gain_rows[:, W * c:W * c + W], start=True, stop=True)
-            if c < 3:
-                nc.scalar.copy(
-                    out=gain_q[:, W * c:W * c + W].rearrange("r (j p) -> r j p", j=4),
-                    in_=bank[:].rearrange("r (p j) -> r j p", j=4),
-                )
-            else:
-                nc.scalar.copy(out=gain_kv[:], in_=bank[:])
+        def spread_gains(b):
+            bank = psum.tile([P, 2, W], BF16, tag="bank", name="gain_bank%d" % b)
+            for m in range(2):
+                cols = slice(W * (2 * b + m), W * (2 * b + m) + W)
+                nc.tensor.matmul(out=bank[:, m, :], lhsT=ones[:], rhs=gain_rows[:, cols], start=True, stop=True)
+            nc.scalar.copy(
+                out=gains[:, 2 * W * b:2 * W * b + 2 * W].bitcast(F32),
+                in_=bank[:].rearrange("p m w -> p (m w)").bitcast(F32),
+            )
 
         cq = {}
         sums = {}
@@ -297,10 +291,7 @@ def tile_mla_model_kernel(
             for c in range(3):
                 cols = slice(W * c, W * c + W)
                 nc.vector.scalar_tensor_tensor(
-                    out=cq[t][:, cols].rearrange("r (j p) -> r j p", j=4),
-                    in0=a_bank[(t, c)][:].rearrange("r (p j) -> r j p", j=4),
-                    scalar=rstd[:, 0:1],
-                    in1=gain_q[:, cols].rearrange("r (j p) -> r j p", j=4),
+                    out=cq[t][:, cols], in0=a_bank[(t, c)][:], scalar=rstd[:, 0:1], in1=gains[:, cols],
                     op0=ALU.mult, op1=ALU.mult,
                 )
 
@@ -310,19 +301,20 @@ def tile_mla_model_kernel(
                 stage1_pass(t, c, g)
 
         def cq_transpose(pair):
-            cq_bank[pair] = psum.tile([P, 8, P], BF16, tag="bank", name="cq_bank%d" % pair)
+            cq_bank[pair] = psum.tile([P, 4, P], F32, tag="bank", name="cq_bank%d" % pair)
             for h in range(2):
                 t, g = divmod(2 * pair + h, 3)
-                for j in range(4):
-                    k0 = 512 * g + P * j
+                words = cq[t][:].bitcast(F32)
+                for u in range(2):
                     nc.tensor.transpose(
-                        out=cq_bank[pair][:, 4 * h + j, :], in_=cq[t][:, k0:k0 + P], identity=ident_bf16[:]
+                        out=cq_bank[pair][:, 2 * h + u, :], in_=words[:, 256 * g + u:256 * g + 256:2],
+                        identity=ident_f32[:],
                     )
 
         def cq_copy(pair):
             cq_grouped[pair] = cqg_pool.tile([P, 2 * W], BF16, tag="cqg", name="cq_grouped%d" % pair, align_bytes=64)
-            dst = cq_grouped[pair][:].rearrange("p (h r j) -> p h r j", h=2, j=4)
-            src = cq_bank[pair][:].rearrange("p (h j) r -> p h r j", h=2)
+            dst = cq_grouped[pair][:].bitcast(F32).rearrange("p (h r u) -> p h r u", h=2, u=2)
+            src = cq_bank[pair][:].rearrange("p (h u) r -> p h r u", h=2)
             if CQ_COPY_ENGINE[pair] == "S":
                 nc.scalar.copy(out=dst, in_=src)
             else:
@@ -355,7 +347,7 @@ def tile_mla_model_kernel(
         def rope_sum(key):
             p1, p2, n, first_slot = products[key]
             slots = out_tile[key][:].rearrange("p (s h w) -> p s h w", h=2, w=HALF)
-            nc.vector.tensor_tensor(out=slots[:, first_slot:8:3], in0=p1[:, 0:n], in1=p2[:, 0:n], op=ALU.add)
+            nc.gpsimd.tensor_tensor(out=slots[:, first_slot:8:3], in0=p1[:, 0:n], in1=p2[:, 0:n], op=ALU.add)
 
         kv_bank = {}
         kv_rms = {}
@@ -386,7 +378,7 @@ def tile_mla_model_kernel(
             out_tile[("kv", t)] = out_pool.tile([P, W], F32, tag="out", name="kv_out%d" % t)
             nc.vector.scalar_tensor_tensor(
                 out=out_tile[("kv", t)][:, 0:KVR], in0=kv_bank[t][:, 0:KVR], scalar=rstd[:, 0:1],
-                in1=gain_kv[:, 0:KVR], op0=ALU.mult, op1=ALU.mult,
+                in1=gains[:, QR:QR + KVR], op0=ALU.mult, op1=ALU.mult,
             )
             rope_products(("kv", t), kv_bank[t], KV_ROPE_SLOT, t)
             rope_sum(("kv", t))
@@ -405,10 +397,10 @@ def tile_mla_model_kernel(
             rope_sum((s, t))
             nc.sync.dma_start(out=out_view[:, t, W * s:W * s + W], in_=out_tile[(s, t)][:])
 
+        regroup_next()
         x_transpose(0)
         x_transpose(1)
         x_quantise(0)
-        regroup_next()
         x_transpose(2)
         x_quantise(1)
         regroup_next()
@@ -418,8 +410,8 @@ def tile_mla_model_kernel(
         x_quantise(2)
         advance()
         x_quantise(3)
-        for c in (3, 0, 1, 2):
-            spread_gains(c)
+        for b in (1, 0):
+            spread_gains(b)
         advance()
         advance()
         for t in range(TILES):

@@ -178,8 +178,9 @@ def tile_mla_model_kernel(
                 return
             done["copied"] = k + 1
             grouped[k] = grouped_pool.tile([P, 4 * W], BF16, tag="grouped", name="grouped%d" % k, align_bytes=64)
-            dst = grouped[k][:].rearrange("p (c i t) -> p c t i", i=4, t=4)
-            src = units[k][0].rearrange("p t (c i) -> p c t i", i=4)
+            run = 8 if COPY_ENGINE[k] == "S" else 4
+            dst = grouped[k][:].rearrange("p (c i t) -> p c t i", i=run, t=4)
+            src = units[k][0].rearrange("p t (c i) -> p c t i", i=run)
             if COPY_ENGINE[k] == "S":
                 nc.scalar.copy(out=dst, in_=src)
             else:

@@ -178,9 +178,8 @@ def tile_mla_model_kernel(
                 return
             done["copied"] = k + 1
             grouped[k] = grouped_pool.tile([P, 4 * W], BF16, tag="grouped", name="grouped%d" % k, align_bytes=64)
-            run = 8 if COPY_ENGINE[k] == "S" else 4
-            dst = grouped[k][:].rearrange("p (c i t) -> p c t i", i=run, t=4)
-            src = units[k][0].rearrange("p t (c i) -> p c t i", i=run)
+            dst = grouped[k][:].rearrange("p (c i t) -> p c t i", i=8, t=4)
+            src = units[k][0].rearrange("p t (c i) -> p c t i", i=8)
             if COPY_ENGINE[k] == "S":
                 nc.scalar.copy(out=dst, in_=src)
             else:

@@ -21,11 +21,13 @@ FLOPS = 2 * T * (H * QR + QR * NQ + H * KV)
 
 EARLY_BANKS = ((0, 0), (0, 1), (0, 2), (1, 0), (1, 1), (1, 2), (2, 0), (2, 1))
 
-COPY_ENGINE = "VSVV" + "VSVSVSVSVSVS" + "SVSSVSSVSVVSSVSSVV"
-CQ_COPY_ENGINE = "SSSSVV"
+COPY_ENGINE = "HHVV" + "VSVSVSVSVSVS" + "VVV" + "SVS" + "SVS" + "VSV" + "SVS" + "VSS"
+CQ_COPY_ENGINE = "SSSSSS"
 
-FIRST_ROPE_SLOT = (2, 0, 1)
-KV_ROPE_SLOT = 7
+ROPE, LOW, HIGH = range(3)
+Q_ORDER = ((0, ROPE), (0, LOW), (0, HIGH), (1, ROPE), (1, LOW), (1, HIGH))
+HEAD = 192
+DN = 128
 
 
 def tile_mla_model_kernel(
@@ -37,14 +39,13 @@ def tile_mla_model_kernel(
         keep = ctx.enter_context(tc.tile_pool(name="keep", bufs=1))
         raw_pool = ctx.enter_context(tc.tile_pool(name="raw", bufs=6))
         code_pool = ctx.enter_context(tc.tile_pool(name="codes", bufs=6))
-        small_raw = ctx.enter_context(tc.tile_pool(name="small_raw", bufs=5))
-        grouped_pool = ctx.enter_context(tc.tile_pool(name="grouped", bufs=6))
-        rope_pool = ctx.enter_context(tc.tile_pool(name="rope", bufs=3))
+        small_pool = ctx.enter_context(tc.tile_pool(name="small", bufs=8))
+        grouped_pool = ctx.enter_context(tc.tile_pool(name="grouped", bufs=5))
+        rope_pool = ctx.enter_context(tc.tile_pool(name="rope", bufs=2))
         junk_pool = ctx.enter_context(tc.tile_pool(name="junk", bufs=2))
         cqg_pool = ctx.enter_context(tc.tile_pool(name="cqg", bufs=4))
         cq_pool = ctx.enter_context(tc.tile_pool(name="cq", bufs=3))
         stat = ctx.enter_context(tc.tile_pool(name="stat", bufs=4))
-        out_pool = ctx.enter_context(tc.tile_pool(name="outp", bufs=7))
         psum = ctx.enter_context(tc.psum_pool(name="psum", bufs=8))
 
         x_view = token_x.rearrange("(p t) h -> p t h", t=TILES)
@@ -67,11 +68,11 @@ def tile_mla_model_kernel(
         wkv_raw = []
 
         def load_x(t):
-            x_raw.append(small_raw.tile([P, H], BF16, tag="small", name="x_raw%d" % t))
+            x_raw.append(small_pool.tile([P, H], BF16, tag="small", name="x_raw%d" % t))
             nc.sync.dma_start(out=x_raw[t][:], in_=x_view[:, t, :])
 
         def load_wkv(g):
-            chunk = small_raw.tile([P, 4, W], BF16, tag="small", name="wkv_raw%d" % g)
+            chunk = small_pool.tile([P, 4, W], BF16, tag="small", name="wkv_raw%d" % g)
             nc.sync.dma_start(
                 out=chunk[:],
                 in_=wkv[512 * g:512 * g + 512, :].rearrange("(p j) c -> p j c", j=4),
@@ -79,27 +80,25 @@ def tile_mla_model_kernel(
             wkv_raw.append(chunk)
 
         load_wkv(0)
+        load_wkv(1)
         load_x(0)
+        load_wkv(2)
         load_x(1)
         nc.sync.dma_start(out=gain_rows[0:1, 0:QR], in_=gamma_cq.unsqueeze(0))
         nc.sync.dma_start(out=gain_rows[0:1, QR:QR + KVR], in_=gamma_ckv.unsqueeze(0))
+        load_wkv(3)
+        load_x(2)
+        load_x(3)
         nc.sync.dma_start(out=cos_raw[:], in_=rope_cos.rearrange("(p t) d -> p t d", t=TILES))
         nc.sync.dma_start(out=sin_raw[:], in_=rope_sin.rearrange("(p t) d -> p t d", t=TILES))
-        load_x(2)
-        load_wkv(1)
-        load_x(3)
-        load_wkv(2)
-        load_wkv(3)
 
-        table_1 = const.tile([P, TILES, DR], F32, name="table_1")
-        table_2 = const.tile([P, TILES, DR], F32, name="table_2")
-        nc.gpsimd.tensor_copy(out=table_1[:, :, 0:HALF], in_=cos_raw[:, :, 0:HALF])
-        nc.gpsimd.tensor_copy(out=table_1[:, :, HALF:DR], in_=sin_raw[:, :, HALF:DR])
+        table = const.tile([P, TILES, 4, HALF], F32, name="table")
+        nc.gpsimd.tensor_copy(out=table[:, :, 0, :], in_=cos_raw[:, :, 0:HALF])
+        nc.gpsimd.tensor_copy(out=table[:, :, 1, :], in_=sin_raw[:, :, HALF:DR])
         nc.gpsimd.tensor_scalar(
-            out=table_2[:, :, 0:HALF], in0=sin_raw[:, :, 0:HALF], scalar1=-1.0, scalar2=0.0,
-            op0=ALU.mult, op1=ALU.add,
+            out=table[:, :, 2, :], in0=sin_raw[:, :, 0:HALF], scalar1=-1.0, scalar2=0.0, op0=ALU.mult, op1=ALU.add
         )
-        nc.gpsimd.tensor_copy(out=table_2[:, :, HALF:DR], in_=cos_raw[:, :, HALF:DR])
+        nc.gpsimd.tensor_copy(out=table[:, :, 3, :], in_=cos_raw[:, :, HALF:DR])
 
         x_codes = keep.tile([P, TILES, W], U32, name="x_codes", align_bytes=64)
         x_scales = keep.tile([P, TILES, W], U8, name="x_scales", align_bytes=64)
@@ -132,28 +131,30 @@ def tile_mla_model_kernel(
                 cols = slice(W * c, W * c + W)
                 units.append((chunk[:, :, cols], wa_codes[g][:, cols], wa_scales[g][:, cols], ("a", g, c)))
         wb_codes, wb_scales = {}, {}
+        wb_units = {}
         for half in range(2):
-            chunks = []
             for g in range(3):
                 chunk = raw_pool.tile([P, 4, QR], BF16, tag="raw", name="wb_raw%d%d" % (half, g))
                 nc.sync.dma_start(
                     out=chunk[:],
                     in_=wq_b[512 * g:512 * g + 512, QR * half:QR * half + QR].rearrange("(p j) n -> p j n", j=4),
                 )
-                chunks.append(chunk)
                 wb_codes[(half, g)] = code_pool.tile(
                     [P, QR], U32, tag="codes", name="wb_codes%d%d" % (half, g), align_bytes=64
                 )
                 wb_scales[(half, g)] = code_pool.tile(
                     [P, QR], U8, tag="scales", name="wb_scales%d%d" % (half, g), align_bytes=64
                 )
-            for c in range(3):
-                cols = slice(W * c, W * c + W)
-                for g in range(3):
-                    units.append((
-                        chunks[g][:, :, cols], wb_codes[(half, g)][:, cols], wb_scales[(half, g)][:, cols],
-                        ("q", 3 * half + c, g),
-                    ))
+                heads = chunk[:].rearrange("p j (h d) -> p j h d", d=HEAD)
+                sources = (heads[:, :, :, DN:HEAD], heads[:, :, 0:4, 0:DN], heads[:, :, 4:8, 0:DN])
+                for part in (ROPE, LOW, HIGH):
+                    cols = slice(W * part, W * part + W)
+                    wb_units[(half, g, part)] = (
+                        sources[part], wb_codes[(half, g)][:, cols], wb_scales[(half, g)][:, cols], None
+                    )
+        for half, part in Q_ORDER:
+            for g in range(3):
+                units.append(wb_units[(half, g, part)])
 
         a_bank = {}
         q_bank = {}
@@ -178,12 +179,19 @@ def tile_mla_model_kernel(
                 return
             done["copied"] = k + 1
             grouped[k] = grouped_pool.tile([P, 4 * W], BF16, tag="grouped", name="grouped%d" % k, align_bytes=64)
-            dst = grouped[k][:].rearrange("p (c i t) -> p c t i", i=8, t=4)
-            src = units[k][0].rearrange("p t (c i) -> p c t i", i=8)
-            if COPY_ENGINE[k] == "S":
-                nc.scalar.copy(out=dst, in_=src)
+            raw = units[k][0]
+            if len(raw.shape) == 4:
+                dst = grouped[k][:].rearrange("p (h c i j) -> p h c j i", h=raw.shape[2], i=8, j=4)
+                src = raw.rearrange("p j h (c i) -> p h c j i", i=8)
             else:
-                nc.vector.tensor_copy(out=dst, in_=src)
+                dst = grouped[k][:].rearrange("p (c i j) -> p c j i", i=8, j=4)
+                src = raw.rearrange("p j (c i) -> p c j i", i=8)
+            n = src.shape[1]
+            split = {"V": n, "S": 0, "H": n // 2}[COPY_ENGINE[k]]
+            if split > 0:
+                nc.vector.tensor_copy(out=dst[:, 0:split], in_=src[:, 0:split])
+            if split < n:
+                nc.scalar.copy(out=dst[:, split:n], in_=src[:, split:n])
 
         def quantise_next():
             k = done["quantised"]
@@ -200,34 +208,44 @@ def tile_mla_model_kernel(
             what = units[k][3]
             if what is None:
                 return
-            if what[0] == "a":
-                g, c = what[1], what[2]
-                for t in range(TILES):
-                    if (t, c) in EARLY_BANKS:
-                        if g == 0:
-                            a_bank[(t, c)] = psum.tile([P, W], F32, tag="bank", name="a%d%d" % (t, c))
-                        stage1_pass(t, c, g)
-            else:
-                s, g = what[1], what[2]
-                half, c = divmod(s, 3)
-                cols = slice(W * c, W * c + W)
-                for t in range(TILES):
+            g, c = what[1], what[2]
+            for t in range(TILES):
+                if (t, c) in EARLY_BANKS and not (t == 2 and g == 3):
                     if g == 0:
-                        q_bank[(s, t)] = psum.tile([P, W], F32, tag="bank", name="q%d%d" % (s, t))
-                    nc.tensor.matmul_mx(
-                        out=q_bank[(s, t)][:],
-                        lhsT=cq_codes[:, t, P * g:P * g + P].bitcast(FP8X4),
-                        lhsT_scale=cq_scales[:, t, P * g:P * g + P],
-                        rhs=wb_codes[(half, g)][:, cols].bitcast(FP8X4),
-                        rhs_scale=wb_scales[(half, g)][:, cols],
-                        start=(g == 0),
-                        stop=(g == 2),
-                    )
+                        a_bank[(t, c)] = psum.tile([P, W], F32, tag="bank", name="a%d%d" % (t, c))
+                    stage1_pass(t, c, g)
 
-        def advance():
-            regroup_next()
-            quantise_next()
-            multiply_next()
+        def q_pass(half, part, t, g):
+            if g == 0:
+                q_bank[(half, part, t)] = psum.tile([P, W], F32, tag="bank", name="q%d%d%d" % (half, part, t))
+            cols = slice(W * part, W * part + W)
+            nc.tensor.matmul_mx(
+                out=q_bank[(half, part, t)][:],
+                lhsT=cq_codes[:, t, P * g:P * g + P].bitcast(FP8X4),
+                lhsT_scale=cq_scales[:, t, P * g:P * g + P],
+                rhs=wb_codes[(half, g)][:, cols].bitcast(FP8X4),
+                rhs_scale=wb_scales[(half, g)][:, cols],
+                start=(g == 0),
+                stop=(g == 2),
+            )
+
+        def q_passes(half, part, t):
+            for g in range(3):
+                q_pass(half, part, t, g)
+
+        def regroup_to(count):
+            while done["copied"] < min(count, len(units)):
+                regroup_next()
+
+        def quantise_to(count):
+            while done["quantised"] < count:
+                quantise_next()
+
+        def advance(ahead, cap=len(COPY_ENGINE)):
+            regroup_to(min(done["quantised"] + 1 + ahead, cap))
+            if done["quantised"] < len(units):
+                quantise_next()
+                multiply_next()
 
         x_grouped = {}
         x_bank = {}
@@ -330,27 +348,24 @@ def tile_mla_model_kernel(
         products = {}
         out_tile = {}
 
-        def rope_products(key, bank, first_slot, t):
-            n = len(range(first_slot, 8, 3))
-            halves = bank[:].rearrange("p (s w) -> p s w", w=HALF)
-            shape = [P, n, 2, HALF]
-            x1 = halves[:, 2 * first_slot:16:6, :].unsqueeze(2).to_broadcast(shape)
-            x2 = halves[:, 2 * first_slot + 1:16:6, :].unsqueeze(2).to_broadcast(shape)
-            t1 = table_1[:, t, :].rearrange("p (h w) -> p h w", h=2).unsqueeze(1).to_broadcast(shape)
-            t2 = table_2[:, t, :].rearrange("p (h w) -> p h w", h=2).unsqueeze(1).to_broadcast(shape)
-            p1 = rope_pool.tile([P, 3, 2, HALF], F32, tag="p1", name="p1")
-            p2 = rope_pool.tile([P, 3, 2, HALF], F32, tag="p2", name="p2")
-            nc.vector.tensor_tensor(out=p1[:, 0:n], in0=x1, in1=t1, op=ALU.mult)
-            nc.vector.tensor_tensor(out=p2[:, 0:n], in0=x2, in1=t2, op=ALU.mult)
-            products[key] = (p1, p2, n, first_slot)
+        def rope_products(key, rope_columns, t):
+            halves = rope_columns.rearrange("p (n h w) -> p n h w", h=2, w=HALF)
+            n = halves.shape[1]
+            shape = [P, n, 2, 2, HALF]
+            product = rope_pool.tile([P, 8, 2, 2, HALF], F32, tag="product", name="product")
+            nc.vector.tensor_tensor(
+                out=product[:, 0:n], in0=halves.unsqueeze(3).to_broadcast(shape),
+                in1=table[:, t].rearrange("p (h d) w -> p h d w", h=2).unsqueeze(1).to_broadcast(shape), op=ALU.mult,
+            )
+            products[key] = product
 
-        def rope_sum(key):
-            p1, p2, n, first_slot = products[key]
-            slots = out_tile[key][:].rearrange("p (s h w) -> p s h w", h=2, w=HALF)
-            nc.gpsimd.tensor_tensor(out=slots[:, first_slot:8:3], in0=p1[:, 0:n], in1=p2[:, 0:n], op=ALU.add)
+        def rope_sum(key, heads, out):
+            product = products[key]
+            nc.gpsimd.tensor_tensor(out=out, in0=product[:, heads, 0], in1=product[:, heads, 1], op=ALU.add)
 
         kv_bank = {}
         kv_rms = {}
+        kv_rstd = {}
 
         def kv_passes(t):
             kv_bank[t] = psum.tile([P, W], F32, tag="bank", name="kv%d" % t)
@@ -365,81 +380,119 @@ def tile_mla_model_kernel(
                     stop=(g == 3),
                 )
 
-        def kv_root_mean_square(t):
-            total = stat.tile([P, 1], F32, tag="total", name="kv_total%d" % t)
-            junk = junk_pool.tile([P, W], BF16, tag="junk", name="junk")
-            nc.scalar.activation(out=junk[:, 0:KVR], in_=kv_bank[t][:, 0:KVR], func=ACT.Square, accum_out=total[:])
-            kv_rms[t] = stat.tile([P, 1], F32, tag="rms", name="kv_rms%d" % t)
-            nc.scalar.activation(out=kv_rms[t][:], in_=total[:], func=ACT.Sqrt, bias=eps[:, 0:1], scale=1.0 / KVR)
+        def kv_root_mean_squares(first):
+            total = stat.tile([P, 2], F32, tag="kv_total", name="kv_total%d" % first)
+            for i in range(2):
+                junk = junk_pool.tile([P, W], BF16, tag="junk", name="junk")
+                nc.scalar.activation(
+                    out=junk[:, 0:KVR], in_=kv_bank[first + i][:, 0:KVR], func=ACT.Square, accum_out=total[:, i:i + 1]
+                )
+            kv_rms[first] = stat.tile([P, 2], F32, tag="kv_rms", name="kv_rms%d" % first)
+            nc.scalar.activation(
+                out=kv_rms[first][:], in_=total[:], func=ACT.Sqrt, bias=eps[:, 0:1], scale=1.0 / KVR
+            )
+
+        def kv_invert(first):
+            rstd = stat.tile([P, 2], F32, tag="kv_rstd", name="kv_rstd%d" % first)
+            nc.vector.reciprocal(out=rstd[:], in_=kv_rms[first][:])
+            for i in range(2):
+                kv_rstd[first + i] = rstd[:, i:i + 1]
 
         def kv_finish(t):
-            rstd = stat.tile([P, 1], F32, tag="rstd", name="kv_rstd%d" % t)
-            nc.vector.reciprocal(out=rstd[:], in_=kv_rms[t][:])
-            out_tile[("kv", t)] = out_pool.tile([P, W], F32, tag="out", name="kv_out%d" % t)
+            out_tile[("kv", t)] = small_pool.tile([P, W], F32, tag="small", name="kv_out%d" % t)
+            rope_products(("kv", t), kv_bank[t][:, KVR:KV], t)
             nc.vector.scalar_tensor_tensor(
-                out=out_tile[("kv", t)][:, 0:KVR], in0=kv_bank[t][:, 0:KVR], scalar=rstd[:, 0:1],
+                out=out_tile[("kv", t)][:, 0:KVR], in0=kv_bank[t][:, 0:KVR], scalar=kv_rstd[t],
                 in1=gains[:, QR:QR + KVR], op0=ALU.mult, op1=ALU.mult,
             )
-            rope_products(("kv", t), kv_bank[t], KV_ROPE_SLOT, t)
-            rope_sum(("kv", t))
+            rope_sum(
+                ("kv", t), slice(0, 1), out_tile[("kv", t)][:, KVR:KV].rearrange("p (n h w) -> p n h w", n=1, h=2)
+            )
             nc.sync.dma_start(out=out_view[:, t, NQ:NQ + KV], in_=out_tile[("kv", t)][:])
 
-        def plain_columns_out(s, t):
-            rope_class = FIRST_ROPE_SLOT[s % 3] % 3
-            out_tile[(s, t)] = out_pool.tile([P, W], F32, tag="out", name="q_out%d%d" % (s, t))
-            src = q_bank[(s, t)][:].rearrange("p (s w) -> p s w", w=DR)
-            dst = out_tile[(s, t)][:].rearrange("p (s w) -> p s w", w=DR)
-            for r in range(3):
-                if r != rope_class:
-                    nc.scalar.copy(out=dst[:, r:8:3, :], in_=src[:, r:8:3, :])
+        def out_of(half, part, t):
+            key = (half, part, t)
+            if key not in out_tile:
+                out_tile[key] = small_pool.tile([P, 4, HEAD], F32, tag="small", name="q_out%d%d%d" % key)
+            return out_tile[key]
 
-        def q_store(s, t):
-            rope_sum((s, t))
-            nc.sync.dma_start(out=out_view[:, t, W * s:W * s + W], in_=out_tile[(s, t)][:])
+        def plain_out(half, part, t, engine):
+            dst = out_of(half, part, t)[:, :, 0:DN]
+            src = q_bank[(half, part, t)][:].rearrange("p (h d) -> p h d", d=DN)
+            if engine == "S":
+                nc.scalar.copy(out=dst, in_=src)
+            else:
+                nc.vector.tensor_copy(out=dst, in_=src)
 
-        regroup_next()
+        def q_rope_products(half, t):
+            rope_products((half, t), q_bank[(half, ROPE, t)][:], t)
+
+        def q_rope_sum(half, part, t):
+            heads = slice(0, 4) if part == LOW else slice(4, 8)
+            dst = out_of(half, part, t)[:, :, DN:HEAD].rearrange("p n (h w) -> p n h w", h=2)
+            rope_sum((half, t), heads, dst)
+
+        def q_store(half, part, t):
+            first = QR * half + (0 if part == LOW else 4 * HEAD)
+            nc.sync.dma_start(
+                out=out_view[:, t, first:first + 4 * HEAD],
+                in_=out_of(half, part, t)[:].rearrange("p h d -> p (h d)"),
+            )
+
+        engines = {mybir.EngineType.PE, mybir.EngineType.Activation, mybir.EngineType.DVE, mybir.EngineType.Pool}
+        ctx.enter_context(tc.manual_schedule(engines=engines))
+        regroup_to(2)
+        quantise_to(1)
         x_transpose(0)
+        regroup_to(3)
         x_transpose(1)
+        quantise_to(2)
         x_quantise(0)
-        x_transpose(2)
-        x_quantise(1)
-        regroup_next()
-        quantise_next()
-        multiply_next()
-        x_transpose(3)
-        x_quantise(2)
-        advance()
-        x_quantise(3)
         for b in (1, 0):
             spread_gains(b)
-        advance()
-        advance()
-        for t in range(TILES):
-            kv_passes(t)
-        advance()
-        kv_root_mean_square(0)
-        kv_root_mean_square(1)
-        advance()
-        kv_root_mean_square(2)
+        regroup_to(4)
+        quantise_to(3)
+        x_transpose(2)
+        x_quantise(1)
+        x_transpose(3)
+        quantise_to(4)
+        for k in range(4):
+            multiply_next()
+        kv_passes(0)
+        kv_passes(1)
+        x_quantise(2)
+        kv_passes(2)
+        regroup_to(6)
+        x_quantise(3)
+        kv_passes(3)
+        quantise_to(5)
+        multiply_next()
+        kv_root_mean_squares(0)
+        kv_root_mean_squares(2)
+        regroup_to(8)
+        quantise_to(6)
+        multiply_next()
+        kv_invert(0)
         kv_finish(0)
-        advance()
-        kv_root_mean_square(3)
         kv_finish(1)
-        advance()
+        quantise_to(7)
+        multiply_next()
+        regroup_to(9)
+        kv_invert(2)
         kv_finish(2)
-        advance()
         kv_finish(3)
-
-        regroup_next()
-        for k in range(7):
-            advance()
+        while done["quantised"] < 16:
+            advance(2, 16)
+        stage1_pass(2, 0, 3)
+        stage1_pass(2, 1, 3)
 
         squares(0, (0, 1, 2))
         root_mean_square(0)
-        quantise_next()
         squares(1, (0, 1, 2))
         root_mean_square(1)
+        regroup_to(17)
         scale_cq(0)
+        quantise_to(17)
         late_bank(2, 2)
         late_bank(3, 0)
         late_bank(3, 1)
@@ -448,41 +501,122 @@ def tile_mla_model_kernel(
         late_bank(3, 2)
         squares(2, (2,))
         root_mean_square(2)
+        regroup_to(18)
         cq_transpose(0)
-        squares(3, (0,))
-        scale_cq(2)
-        squares(3, (1, 2))
-        root_mean_square(3)
         cq_transpose(1)
+        squares(3, (0, 1))
+        scale_cq(2)
+        quantise_to(18)
         cq_transpose(2)
+        squares(3, (2,))
+        root_mean_square(3)
         cq_copy(0)
+        cq_copy(1)
+        cq_copy(2)
+        cq_quantise(0)
         scale_cq(3)
         cq_transpose(3)
-        cq_copy(1)
-        cq_quantise(0)
         cq_transpose(4)
         cq_transpose(5)
-        cq_copy(2)
-        cq_copy(4)
         cq_quantise(1)
-        cq_copy(3)
-        cq_copy(5)
         cq_quantise(2)
-        cq_quantise(4)
+        regroup_to(19)
+        cq_copy(3)
+        cq_copy(4)
+        cq_copy(5)
         cq_quantise(3)
+        quantise_to(19)
+        cq_quantise(4)
         cq_quantise(5)
-        multiply_next()
-        advance()
-        advance()
 
-        banks = [(s, t) for s in range(6) for t in range(TILES)]
-        for n in range(len(banks) + 2):
-            if n < len(banks):
-                plain_columns_out(*banks[n])
-            if 1 <= n <= len(banks):
-                s, t = banks[n - 1]
-                rope_products((s, t), q_bank[(s, t)], FIRST_ROPE_SLOT[s % 3], t)
-            if n >= 2:
-                q_store(*banks[n - 2])
-            if n % 4 != 3:
-                advance()
+        regroup_to(21)
+        for t in range(TILES):
+            q_passes(0, ROPE, t)
+        regroup_to(22)
+        quantise_to(20)
+        regroup_to(23)
+        quantise_to(21)
+        q_rope_products(0, 0)
+        quantise_to(22)
+        for t in range(2):
+            q_passes(0, LOW, t)
+        q_rope_products(0, 1)
+        regroup_to(24)
+        quantise_to(23)
+        for t in range(2, TILES):
+            q_passes(0, LOW, t)
+        q_rope_sum(0, LOW, 0)
+        q_rope_sum(0, HIGH, 0)
+        q_rope_sum(0, LOW, 1)
+        q_rope_sum(0, HIGH, 1)
+        plain_out(0, LOW, 0, "S")
+        q_store(0, LOW, 0)
+        plain_out(0, LOW, 1, "S")
+        q_store(0, LOW, 1)
+        regroup_to(25)
+        quantise_to(24)
+        q_rope_products(0, 2)
+        quantise_to(25)
+        for t in range(TILES):
+            q_passes(0, HIGH, t)
+        regroup_to(27)
+        q_rope_products(0, 3)
+        q_rope_sum(0, LOW, 2)
+        q_rope_sum(0, HIGH, 2)
+        q_rope_sum(0, LOW, 3)
+        q_rope_sum(0, HIGH, 3)
+        plain_out(0, LOW, 2, "S")
+        q_store(0, LOW, 2)
+        plain_out(0, LOW, 3, "S")
+        q_store(0, LOW, 3)
+        quantise_to(26)
+        regroup_to(28)
+        quantise_to(28)
+        for t in range(TILES):
+            q_passes(1, ROPE, t)
+        regroup_to(29)
+        for t in range(2):
+            plain_out(0, HIGH, t, "S")
+            q_store(0, HIGH, t)
+        quantise_to(29)
+        regroup_to(30)
+        quantise_to(30)
+        regroup_to(31)
+        for t in range(2, TILES):
+            plain_out(0, HIGH, t, "S")
+            q_store(0, HIGH, t)
+        quantise_to(31)
+        for t in range(TILES):
+            q_passes(1, LOW, t)
+        q_rope_products(1, 0)
+        q_rope_sum(1, LOW, 0)
+        q_rope_sum(1, HIGH, 0)
+        regroup_to(33)
+        quantise_to(32)
+        q_rope_products(1, 1)
+        q_rope_sum(1, LOW, 1)
+        q_rope_sum(1, HIGH, 1)
+        for t in range(2):
+            plain_out(1, LOW, t, "S")
+            q_store(1, LOW, t)
+        regroup_to(34)
+        quantise_to(33)
+        for g in range(2):
+            for t in range(TILES):
+                q_pass(1, HIGH, t, g)
+        q_rope_products(1, 2)
+        q_rope_sum(1, LOW, 2)
+        q_rope_sum(1, HIGH, 2)
+        for t in range(2, TILES):
+            plain_out(1, LOW, t, "S")
+        q_store(1, LOW, 2)
+        quantise_to(34)
+        for t in range(TILES):
+            q_pass(1, HIGH, t, 2)
+        q_rope_products(1, 3)
+        q_rope_sum(1, LOW, 3)
+        q_store(1, LOW, 3)
+        q_rope_sum(1, HIGH, 3)
+        for t in range(TILES):
+            plain_out(1, HIGH, t, "SVSV"[t])
+            q_store(1, HIGH, t)

from contextlib import ExitStack

import concourse.mybir as mybir
from concourse.masks import make_identity

F32 = mybir.dt.float32
BF16 = mybir.dt.bfloat16
U32 = mybir.dt.uint32
U8 = mybir.dt.uint8
FP8X4 = mybir.dt.float8_e4m3fn_x4
ALU = mybir.AluOpType
ACT = mybir.ActivationFunctionType

P = 128
TILES = 4
T, H, QR, NQ, KV, KVR, DR = 512, 2048, 1536, 3072, 512, 448, 64
HALF = DR // 2
W = 512
EPS = 1e-6
FLOPS = 2 * T * (H * QR + QR * NQ + H * KV)

EARLY_BANKS = ((0, 0), (0, 1), (0, 2), (1, 0), (1, 1), (1, 2), (2, 0), (2, 1))

COPY_ENGINE = "HHVV" + "VSVSVSVSVSVS" + "VVV" + "SVS" + "SVS" + "VSV" + "SVS" + "VSS"
CQ_COPY_ENGINE = "SSSSSS"

ROPE, LOW, HIGH = range(3)
Q_ORDER = ((0, ROPE), (0, LOW), (0, HIGH), (1, ROPE), (1, LOW), (1, HIGH))
HEAD = 192
DN = 128


def tile_mla_model_kernel(
    tc, token_x, wq_a, wq_b, wkv, rope_cos, rope_sin, gamma_cq, gamma_ckv, out
):
    nc = tc.nc
    with ExitStack() as ctx:
        const = ctx.enter_context(tc.tile_pool(name="const", bufs=1))
        keep = ctx.enter_context(tc.tile_pool(name="keep", bufs=1))
        raw_pool = ctx.enter_context(tc.tile_pool(name="raw", bufs=6))
        code_pool = ctx.enter_context(tc.tile_pool(name="codes", bufs=6))
        small_pool = ctx.enter_context(tc.tile_pool(name="small", bufs=8))
        grouped_pool = ctx.enter_context(tc.tile_pool(name="grouped", bufs=5))
        rope_pool = ctx.enter_context(tc.tile_pool(name="rope", bufs=2))
        junk_pool = ctx.enter_context(tc.tile_pool(name="junk", bufs=2))
        cqg_pool = ctx.enter_context(tc.tile_pool(name="cqg", bufs=4))
        cq_pool = ctx.enter_context(tc.tile_pool(name="cq", bufs=3))
        stat = ctx.enter_context(tc.tile_pool(name="stat", bufs=4))
        psum = ctx.enter_context(tc.psum_pool(name="psum", bufs=8))

        x_view = token_x.rearrange("(p t) h -> p t h", t=TILES)
        out_view = out.rearrange("(p t) n -> p t n", t=TILES)

        eps = const.tile([P, 1], F32, name="eps")
        nc.vector.memset(eps[:], EPS)
        gain_rows = grouped_pool.tile([P, 4 * W], BF16, tag="grouped", name="gain_rows", align_bytes=64)
        nc.vector.memset(gain_rows[:], 0.0)
        ones = const.tile([P, P], BF16, name="ones")
        nc.vector.memset(ones[:], 1.0)
        cos_raw = const.tile([P, TILES, DR], BF16, name="cos_raw")
        sin_raw = const.tile([P, TILES, DR], BF16, name="sin_raw")
        warm = const.tile([P, 1], F32, name="warm")
        nc.scalar.activation(out=warm[:], in_=eps[:], func=ACT.Sqrt)
        ident_f32 = const.tile([P, P], F32, name="ident_f32")
        make_identity(nc, ident_f32[:])

        x_raw = []
        wkv_raw = []

        def load_x(t):
            x_raw.append(small_pool.tile([P, H], BF16, tag="small", name="x_raw%d" % t))
            nc.sync.dma_start(out=x_raw[t][:], in_=x_view[:, t, :])

        def load_wkv(g):
            chunk = small_pool.tile([P, 4, W], BF16, tag="small", name="wkv_raw%d" % g)
            nc.sync.dma_start(
                out=chunk[:],
                in_=wkv[512 * g:512 * g + 512, :].rearrange("(p j) c -> p j c", j=4),
            )
            wkv_raw.append(chunk)

        load_wkv(0)
        load_wkv(1)
        load_x(0)
        load_wkv(2)
        load_x(1)
        nc.sync.dma_start(out=gain_rows[0:1, 0:QR], in_=gamma_cq.unsqueeze(0))
        nc.sync.dma_start(out=gain_rows[0:1, QR:QR + KVR], in_=gamma_ckv.unsqueeze(0))
        load_wkv(3)
        load_x(2)
        load_x(3)
        nc.sync.dma_start(out=cos_raw[:], in_=rope_cos.rearrange("(p t) d -> p t d", t=TILES))
        nc.sync.dma_start(out=sin_raw[:], in_=rope_sin.rearrange("(p t) d -> p t d", t=TILES))

        table = const.tile([P, TILES, 4, HALF], F32, name="table")
        nc.gpsimd.tensor_copy(out=table[:, :, 0, :], in_=cos_raw[:, :, 0:HALF])
        nc.gpsimd.tensor_copy(out=table[:, :, 1, :], in_=sin_raw[:, :, HALF:DR])
        nc.gpsimd.tensor_scalar(
            out=table[:, :, 2, :], in0=sin_raw[:, :, 0:HALF], scalar1=-1.0, scalar2=0.0, op0=ALU.mult, op1=ALU.add
        )
        nc.gpsimd.tensor_copy(out=table[:, :, 3, :], in_=cos_raw[:, :, HALF:DR])

        x_codes = keep.tile([P, TILES, W], U32, name="x_codes", align_bytes=64)
        x_scales = keep.tile([P, TILES, W], U8, name="x_scales", align_bytes=64)
        wkv_codes = keep.tile([P, 4, W], U32, name="wkv_codes", align_bytes=64)
        wkv_scales = keep.tile([P, 4, W], U8, name="wkv_scales", align_bytes=64)
        cq_codes = keep.tile([P, TILES, 3 * P], U32, name="cq_codes", align_bytes=64)
        cq_scales = keep.tile([P, TILES, 3 * P], U8, name="cq_scales", align_bytes=64)
        gains = const.tile([P, 4 * W], BF16, name="gains")

        units = []
        for g in range(4):
            units.append((wkv_raw[g][:], wkv_codes[:, g, :], wkv_scales[:, g, :], None))
        wa_codes, wa_scales = [], []
        for g in range(4):
            chunk = raw_pool.tile([P, 4, QR], BF16, tag="raw", name="wa_raw%d" % g)
            if g == 0:
                for c in range(3):
                    nc.sync.dma_start(
                        out=chunk[:, :, W * c:W * c + W],
                        in_=wq_a[0:512, W * c:W * c + W].rearrange("(p j) c -> p j c", j=4),
                    )
            else:
                nc.sync.dma_start(
                    out=chunk[:],
                    in_=wq_a[512 * g:512 * g + 512, :].rearrange("(p j) c -> p j c", j=4),
                )
            wa_codes.append(code_pool.tile([P, QR], U32, tag="codes", name="wa_codes%d" % g, align_bytes=64))
            wa_scales.append(code_pool.tile([P, QR], U8, tag="scales", name="wa_scales%d" % g, align_bytes=64))
            for c in range(3):
                cols = slice(W * c, W * c + W)
                units.append((chunk[:, :, cols], wa_codes[g][:, cols], wa_scales[g][:, cols], ("a", g, c)))
        wb_codes, wb_scales = {}, {}
        wb_units = {}
        for half in range(2):
            for g in range(3):
                chunk = raw_pool.tile([P, 4, QR], BF16, tag="raw", name="wb_raw%d%d" % (half, g))
                nc.sync.dma_start(
                    out=chunk[:],
                    in_=wq_b[512 * g:512 * g + 512, QR * half:QR * half + QR].rearrange("(p j) n -> p j n", j=4),
                )
                wb_codes[(half, g)] = code_pool.tile(
                    [P, QR], U32, tag="codes", name="wb_codes%d%d" % (half, g), align_bytes=64
                )
                wb_scales[(half, g)] = code_pool.tile(
                    [P, QR], U8, tag="scales", name="wb_scales%d%d" % (half, g), align_bytes=64
                )
                heads = chunk[:].rearrange("p j (h d) -> p j h d", d=HEAD)
                sources = (heads[:, :, :, DN:HEAD], heads[:, :, 0:4, 0:DN], heads[:, :, 4:8, 0:DN])
                for part in (ROPE, LOW, HIGH):
                    cols = slice(W * part, W * part + W)
                    wb_units[(half, g, part)] = (
                        sources[part], wb_codes[(half, g)][:, cols], wb_scales[(half, g)][:, cols], None
                    )
        for half, part in Q_ORDER:
            for g in range(3):
                units.append(wb_units[(half, g, part)])

        a_bank = {}
        q_bank = {}
        grouped = {}
        done = {"copied": 0, "quantised": 0, "multiplied": 0}

        def stage1_pass(t, c, g):
            cols = slice(W * c, W * c + W)
            nc.tensor.matmul_mx(
                out=a_bank[(t, c)][:],
                lhsT=x_codes[:, t, P * g:P * g + P].bitcast(FP8X4),
                lhsT_scale=x_scales[:, t, P * g:P * g + P],
                rhs=wa_codes[g][:, cols].bitcast(FP8X4),
                rhs_scale=wa_scales[g][:, cols],
                start=(g == 0),
                stop=(g == 3),
            )

        def regroup_next():
            k = done["copied"]
            if k >= len(units):
                return
            done["copied"] = k + 1
            grouped[k] = grouped_pool.tile([P, 4 * W], BF16, tag="grouped", name="grouped%d" % k, align_bytes=64)
            raw = units[k][0]
            if len(raw.shape) == 4:
                dst = grouped[k][:].rearrange("p (h c i j) -> p h c j i", h=raw.shape[2], i=8, j=4)
                src = raw.rearrange("p j h (c i) -> p h c j i", i=8)
            else:
                dst = grouped[k][:].rearrange("p (c i j) -> p c j i", i=8, j=4)
                src = raw.rearrange("p j (c i) -> p c j i", i=8)
            n = src.shape[1]
            split = {"V": n, "S": 0, "H": n // 2}[COPY_ENGINE[k]]
            if split > 0:
                nc.vector.tensor_copy(out=dst[:, 0:split], in_=src[:, 0:split])
            if split < n:
                nc.scalar.copy(out=dst[:, split:n], in_=src[:, split:n])

        def quantise_next():
            k = done["quantised"]
            if k >= len(units):
                return
            done["quantised"] = k + 1
            nc.vector.quantize_mx(out=units[k][1].bitcast(FP8X4), scales=units[k][2], in_=grouped[k][:])

        def multiply_next():
            k = done["multiplied"]
            if k >= len(units):
                return
            done["multiplied"] = k + 1
            what = units[k][3]
            if what is None:
                return
            g, c = what[1], what[2]
            for t in range(TILES):
                if (t, c) in EARLY_BANKS and not (t == 2 and g == 3):
                    if g == 0:
                        a_bank[(t, c)] = psum.tile([P, W], F32, tag="bank", name="a%d%d" % (t, c))
                    stage1_pass(t, c, g)

        def q_pass(half, part, t, g):
            if g == 0:
                q_bank[(half, part, t)] = psum.tile([P, W], F32, tag="bank", name="q%d%d%d" % (half, part, t))
            cols = slice(W * part, W * part + W)
            nc.tensor.matmul_mx(
                out=q_bank[(half, part, t)][:],
                lhsT=cq_codes[:, t, P * g:P * g + P].bitcast(FP8X4),
                lhsT_scale=cq_scales[:, t, P * g:P * g + P],
                rhs=wb_codes[(half, g)][:, cols].bitcast(FP8X4),
                rhs_scale=wb_scales[(half, g)][:, cols],
                start=(g == 0),
                stop=(g == 2),
            )

        def q_passes(half, part, t):
            for g in range(3):
                q_pass(half, part, t, g)

        def regroup_to(count):
            while done["copied"] < min(count, len(units)):
                regroup_next()

        def quantise_to(count):
            while done["quantised"] < count:
                quantise_next()

        def advance(ahead, cap=len(COPY_ENGINE)):
            regroup_to(min(done["quantised"] + 1 + ahead, cap))
            if done["quantised"] < len(units):
                quantise_next()
                multiply_next()

        x_grouped = {}
        x_bank = {}

        def x_transpose(t):
            words = x_raw[t][:].bitcast(F32)
            x_grouped[t] = grouped_pool.tile([P, 4 * W], BF16, tag="grouped", name="x_grouped%d" % t, align_bytes=64)
            for pair in range(2):
                x_bank[(t, pair)] = psum.tile([P, 4, P], F32, tag="bank", name="x_bank%d%d" % (t, pair))
                for i in range(4):
                    g, u = divmod(i, 2)
                    w0 = W * pair + 2 * P * g
                    nc.tensor.transpose(
                        out=x_bank[(t, pair)][:, i, :], in_=words[:, w0 + u:w0 + 2 * P:2], identity=ident_f32[:]
                    )
            for pair in range(2):
                dst = x_grouped[t][:].bitcast(F32)[:, W * pair:W * pair + W].rearrange("p (g r u) -> p g r u", g=2, u=2)
                nc.scalar.copy(out=dst, in_=x_bank[(t, pair)][:].rearrange("p (g u) r -> p g r u", u=2))

        def x_quantise(t):
            nc.vector.quantize_mx(out=x_codes[:, t, :].bitcast(FP8X4), scales=x_scales[:, t, :], in_=x_grouped[t][:])

        def spread_gains(b):
            bank = psum.tile([P, 2, W], BF16, tag="bank", name="gain_bank%d" % b)
            for m in range(2):
                cols = slice(W * (2 * b + m), W * (2 * b + m) + W)
                nc.tensor.matmul(out=bank[:, m, :], lhsT=ones[:], rhs=gain_rows[:, cols], start=True, stop=True)
            nc.scalar.copy(
                out=gains[:, 2 * W * b:2 * W * b + 2 * W].bitcast(F32),
                in_=bank[:].rearrange("p m w -> p (m w)").bitcast(F32),
            )

        cq = {}
        sums = {}
        rms = {}
        cq_bank = {}
        cq_grouped = {}
        cq_codes_flat = cq_codes[:].rearrange("p t w -> p (t w)")
        cq_scales_flat = cq_scales[:].rearrange("p t w -> p (t w)")

        def squares(t, thirds):
            if t not in sums:
                sums[t] = stat.tile([P, 4], F32, tag="sums", name="sums%d" % t)
            for c in thirds:
                junk = junk_pool.tile([P, W], BF16, tag="junk", name="junk")
                nc.scalar.activation(
                    out=junk[:], in_=a_bank[(t, c)][:], func=ACT.Square, accum_out=sums[t][:, c:c + 1]
                )

        def root_mean_square(t):
            total = stat.tile([P, 1], F32, tag="total", name="total%d" % t)
            copy3 = stat.tile([P, 4], F32, tag="copy3", name="copy3")
            nc.scalar.activation(out=copy3[:, 0:3], in_=sums[t][:, 0:3], func=ACT.Copy, accum_out=total[:])
            rms[t] = stat.tile([P, 1], F32, tag="rms", name="rms%d" % t)
            nc.scalar.activation(out=rms[t][:], in_=total[:], func=ACT.Sqrt, bias=eps[:, 0:1], scale=1.0 / QR)

        def scale_cq(t):
            rstd = stat.tile([P, 1], F32, tag="rstd", name="rstd%d" % t)
            nc.vector.reciprocal(out=rstd[:], in_=rms[t][:])
            cq[t] = cq_pool.tile([P, QR], BF16, tag="cq", name="cq%d" % t)
            for c in range(3):
                cols = slice(W * c, W * c + W)
                nc.vector.scalar_tensor_tensor(
                    out=cq[t][:, cols], in0=a_bank[(t, c)][:], scalar=rstd[:, 0:1], in1=gains[:, cols],
                    op0=ALU.mult, op1=ALU.mult,
                )

        def late_bank(t, c):
            a_bank[(t, c)] = psum.tile([P, W], F32, tag="bank", name="a%d%d" % (t, c))
            for g in range(4):
                stage1_pass(t, c, g)

        def cq_transpose(pair):
            cq_bank[pair] = psum.tile([P, 4, P], F32, tag="bank", name="cq_bank%d" % pair)
            for h in range(2):
                t, g = divmod(2 * pair + h, 3)
                words = cq[t][:].bitcast(F32)
                for u in range(2):
                    nc.tensor.transpose(
                        out=cq_bank[pair][:, 2 * h + u, :], in_=words[:, 256 * g + u:256 * g + 256:2],
                        identity=ident_f32[:],
                    )

        def cq_copy(pair):
            cq_grouped[pair] = cqg_pool.tile([P, 2 * W], BF16, tag="cqg", name="cq_grouped%d" % pair, align_bytes=64)
            dst = cq_grouped[pair][:].bitcast(F32).rearrange("p (h r u) -> p h r u", h=2, u=2)
            src = cq_bank[pair][:].rearrange("p (h u) r -> p h r u", h=2)
            if CQ_COPY_ENGINE[pair] == "S":
                nc.scalar.copy(out=dst, in_=src)
            else:
                nc.vector.tensor_copy(out=dst, in_=src)

        def cq_quantise(pair):
            nc.vector.quantize_mx(
                out=cq_codes_flat[:, 2 * P * pair:2 * P * pair + 2 * P].bitcast(FP8X4),
                scales=cq_scales_flat[:, 2 * P * pair:2 * P * pair + 2 * P],
                in_=cq_grouped[pair][:],
            )

        products = {}
        out_tile = {}

        def rope_products(key, rope_columns, t):
            halves = rope_columns.rearrange("p (n h w) -> p n h w", h=2, w=HALF)
            n = halves.shape[1]
            shape = [P, n, 2, 2, HALF]
            product = rope_pool.tile([P, 8, 2, 2, HALF], F32, tag="product", name="product")
            nc.vector.tensor_tensor(
                out=product[:, 0:n], in0=halves.unsqueeze(3).to_broadcast(shape),
                in1=table[:, t].rearrange("p (h d) w -> p h d w", h=2).unsqueeze(1).to_broadcast(shape), op=ALU.mult,
            )
            products[key] = product

        def rope_sum(key, heads, out):
            product = products[key]
            nc.gpsimd.tensor_tensor(out=out, in0=product[:, heads, 0], in1=product[:, heads, 1], op=ALU.add)

        kv_bank = {}
        kv_rms = {}
        kv_rstd = {}

        def kv_passes(t):
            kv_bank[t] = psum.tile([P, W], F32, tag="bank", name="kv%d" % t)
            for g in range(4):
                nc.tensor.matmul_mx(
                    out=kv_bank[t][:],
                    lhsT=x_codes[:, t, P * g:P * g + P].bitcast(FP8X4),
                    lhsT_scale=x_scales[:, t, P * g:P * g + P],
                    rhs=wkv_codes[:, g, :].bitcast(FP8X4),
                    rhs_scale=wkv_scales[:, g, :],
                    start=(g == 0),
                    stop=(g == 3),
                )

        def kv_root_mean_squares(first):
            total = stat.tile([P, 2], F32, tag="kv_total", name="kv_total%d" % first)
            for i in range(2):
                junk = junk_pool.tile([P, W], BF16, tag="junk", name="junk")
                nc.scalar.activation(
                    out=junk[:, 0:KVR], in_=kv_bank[first + i][:, 0:KVR], func=ACT.Square, accum_out=total[:, i:i + 1]
                )
            kv_rms[first] = stat.tile([P, 2], F32, tag="kv_rms", name="kv_rms%d" % first)
            nc.scalar.activation(
                out=kv_rms[first][:], in_=total[:], func=ACT.Sqrt, bias=eps[:, 0:1], scale=1.0 / KVR
            )

        def kv_invert(first):
            rstd = stat.tile([P, 2], F32, tag="kv_rstd", name="kv_rstd%d" % first)
            nc.vector.reciprocal(out=rstd[:], in_=kv_rms[first][:])
            for i in range(2):
                kv_rstd[first + i] = rstd[:, i:i + 1]

        def kv_finish(t):
            out_tile[("kv", t)] = small_pool.tile([P, W], F32, tag="small", name="kv_out%d" % t)
            rope_products(("kv", t), kv_bank[t][:, KVR:KV], t)
            nc.vector.scalar_tensor_tensor(
                out=out_tile[("kv", t)][:, 0:KVR], in0=kv_bank[t][:, 0:KVR], scalar=kv_rstd[t],
                in1=gains[:, QR:QR + KVR], op0=ALU.mult, op1=ALU.mult,
            )
            rope_sum(
                ("kv", t), slice(0, 1), out_tile[("kv", t)][:, KVR:KV].rearrange("p (n h w) -> p n h w", n=1, h=2)
            )
            nc.sync.dma_start(out=out_view[:, t, NQ:NQ + KV], in_=out_tile[("kv", t)][:])

        def out_of(half, part, t):
            key = (half, part, t)
            if key not in out_tile:
                out_tile[key] = small_pool.tile([P, 4, HEAD], F32, tag="small", name="q_out%d%d%d" % key)
            return out_tile[key]

        def plain_out(half, part, t, engine):
            dst = out_of(half, part, t)[:, :, 0:DN]
            src = q_bank[(half, part, t)][:].rearrange("p (h d) -> p h d", d=DN)
            if engine == "S":
                nc.scalar.copy(out=dst, in_=src)
            else:
                nc.vector.tensor_copy(out=dst, in_=src)

        def q_rope_products(half, t):
            rope_products((half, t), q_bank[(half, ROPE, t)][:], t)

        def q_rope_sum(half, part, t):
            heads = slice(0, 4) if part == LOW else slice(4, 8)
            dst = out_of(half, part, t)[:, :, DN:HEAD].rearrange("p n (h w) -> p n h w", h=2)
            rope_sum((half, t), heads, dst)

        def q_store(half, part, t):
            first = QR * half + (0 if part == LOW else 4 * HEAD)
            nc.sync.dma_start(
                out=out_view[:, t, first:first + 4 * HEAD],
                in_=out_of(half, part, t)[:].rearrange("p h d -> p (h d)"),
            )

        engines = {mybir.EngineType.PE, mybir.EngineType.Activation, mybir.EngineType.DVE, mybir.EngineType.Pool}
        ctx.enter_context(tc.manual_schedule(engines=engines))
        regroup_to(2)
        quantise_to(1)
        x_transpose(0)
        regroup_to(3)
        x_transpose(1)
        quantise_to(2)
        x_quantise(0)
        for b in (1, 0):
            spread_gains(b)
        regroup_to(4)
        quantise_to(3)
        x_transpose(2)
        x_quantise(1)
        x_transpose(3)
        quantise_to(4)
        for k in range(4):
            multiply_next()
        kv_passes(0)
        kv_passes(1)
        x_quantise(2)
        kv_passes(2)
        regroup_to(6)
        x_quantise(3)
        kv_passes(3)
        quantise_to(5)
        multiply_next()
        kv_root_mean_squares(0)
        kv_root_mean_squares(2)
        regroup_to(8)
        quantise_to(6)
        multiply_next()
        kv_invert(0)
        kv_finish(0)
        kv_finish(1)
        quantise_to(7)
        multiply_next()
        regroup_to(9)
        kv_invert(2)
        kv_finish(2)
        kv_finish(3)
        while done["quantised"] < 16:
            advance(2, 16)
        stage1_pass(2, 0, 3)
        stage1_pass(2, 1, 3)

        squares(0, (0, 1, 2))
        root_mean_square(0)
        squares(1, (0, 1, 2))
        root_mean_square(1)
        regroup_to(17)
        scale_cq(0)
        quantise_to(17)
        late_bank(2, 2)
        late_bank(3, 0)
        late_bank(3, 1)
        squares(2, (0, 1))
        scale_cq(1)
        late_bank(3, 2)
        squares(2, (2,))
        root_mean_square(2)
        regroup_to(18)
        cq_transpose(0)
        cq_transpose(1)
        squares(3, (0, 1))
        scale_cq(2)
        quantise_to(18)
        cq_transpose(2)
        squares(3, (2,))
        root_mean_square(3)
        cq_copy(0)
        cq_copy(1)
        cq_copy(2)
        cq_quantise(0)
        scale_cq(3)
        cq_transpose(3)
        cq_transpose(4)
        cq_transpose(5)
        cq_quantise(1)
        cq_quantise(2)
        regroup_to(19)
        cq_copy(3)
        cq_copy(4)
        cq_copy(5)
        cq_quantise(3)
        quantise_to(19)
        cq_quantise(4)
        cq_quantise(5)

        regroup_to(21)
        for t in range(TILES):
            q_passes(0, ROPE, t)
        regroup_to(22)
        quantise_to(20)
        regroup_to(23)
        quantise_to(21)
        q_rope_products(0, 0)
        quantise_to(22)
        for t in range(2):
            q_passes(0, LOW, t)
        q_rope_products(0, 1)
        regroup_to(24)
        quantise_to(23)
        for t in range(2, TILES):
            q_passes(0, LOW, t)
        q_rope_sum(0, LOW, 0)
        q_rope_sum(0, HIGH, 0)
        q_rope_sum(0, LOW, 1)
        q_rope_sum(0, HIGH, 1)
        plain_out(0, LOW, 0, "S")
        q_store(0, LOW, 0)
        plain_out(0, LOW, 1, "S")
        q_store(0, LOW, 1)
        regroup_to(25)
        quantise_to(24)
        q_rope_products(0, 2)
        quantise_to(25)
        for t in range(TILES):
            q_passes(0, HIGH, t)
        regroup_to(27)
        q_rope_products(0, 3)
        q_rope_sum(0, LOW, 2)
        q_rope_sum(0, HIGH, 2)
        q_rope_sum(0, LOW, 3)
        q_rope_sum(0, HIGH, 3)
        plain_out(0, LOW, 2, "S")
        q_store(0, LOW, 2)
        plain_out(0, LOW, 3, "S")
        q_store(0, LOW, 3)
        quantise_to(26)
        regroup_to(28)
        quantise_to(28)
        for t in range(TILES):
            q_passes(1, ROPE, t)
        regroup_to(29)
        for t in range(2):
            plain_out(0, HIGH, t, "S")
            q_store(0, HIGH, t)
        quantise_to(29)
        regroup_to(30)
        quantise_to(30)
        regroup_to(31)
        for t in range(2, TILES):
            plain_out(0, HIGH, t, "S")
            q_store(0, HIGH, t)
        quantise_to(31)
        for t in range(TILES):
            q_passes(1, LOW, t)
        q_rope_products(1, 0)
        q_rope_sum(1, LOW, 0)
        q_rope_sum(1, HIGH, 0)
        regroup_to(33)
        quantise_to(32)
        q_rope_products(1, 1)
        q_rope_sum(1, LOW, 1)
        q_rope_sum(1, HIGH, 1)
        for t in range(2):
            plain_out(1, LOW, t, "S")
            q_store(1, LOW, t)
        regroup_to(34)
        quantise_to(33)
        for g in range(2):
            for t in range(TILES):
                q_pass(1, HIGH, t, g)
        q_rope_products(1, 2)
        q_rope_sum(1, LOW, 2)
        q_rope_sum(1, HIGH, 2)
        for t in range(2, TILES):
            plain_out(1, LOW, t, "S")
        q_store(1, LOW, 2)
        quantise_to(34)
        for t in range(TILES):
            q_pass(1, HIGH, t, 2)
        q_rope_products(1, 3)
        q_rope_sum(1, LOW, 3)
        q_store(1, LOW, 3)
        q_rope_sum(1, HIGH, 3)
        for t in range(TILES):
            plain_out(1, HIGH, t, "SVSV"[t])
            q_store(1, HIGH, t)
